import numpy as np
import ml_dtypes


def mxq(x, axis, fmt="e4m3"):
    dtype, down = {"e4m3": (ml_dtypes.float8_e4m3fn, 7), "e5m2": (ml_dtypes.float8_e5m2, 14)}[fmt]
    v = np.moveaxis(np.asarray(x, np.float32).astype(ml_dtypes.bfloat16).astype(np.float64), axis, -1)
    blocks = v.reshape(v.shape[:-1] + (-1, 32))
    amax = np.abs(blocks).max(-1, keepdims=True)
    byte = np.maximum(np.where(amax > 0, np.frexp(amax)[1] - 1 + 127, 0) - down, 1)
    scale = np.exp2(byte - 127.0)
    codes = (blocks / scale).astype(np.float32).astype(dtype).astype(np.float64)
    return np.moveaxis((codes * scale).reshape(v.shape), -1, axis)


WIDE = False


def mx_kscale(k):
    if not WIDE:
        return np.ones(k)
    levels = np.array([10, -10, 5, -5, 0])
    a = np.random.permutation(np.resize(levels, k // 512 * 4)).reshape(k // 512, 4)
    idx = np.arange(k)
    return np.exp2(a[idx // 512, idx % 128 // 32])


BF16 = ml_dtypes.bfloat16


def bf(x):
    return np.asarray(x, np.float32).astype(BF16)


def f64(x):
    return np.asarray(x).astype(np.float64)


E2M1 = np.array([0.0, 0.5, 1.0, 1.5, 2.0, 3.0, 4.0, 6.0, -0.0, -0.5, -1.0, -1.5, -2.0, -3.0, -4.0, -6.0])


def pack_weight(w, fmt):
    k, n = w.shape
    w = f64(bf(w)).reshape(k // 32, 32, n)
    amax = np.abs(w).max(1)
    if fmt == "e4m3":
        byte = np.frexp(amax)[1] - 1 + 127 - 7
    else:
        mant, ex = np.frexp(amax / 6.0)
        byte = np.where(mant > 0.5, ex, ex - 1) + 127
    byte = np.clip(np.where(amax > 0, byte, 1), 1, 254)
    scaled = (w * np.exp2(127.0 - byte)[:, None, :]).reshape(k, n).astype(np.float32)
    by_word = np.ascontiguousarray(scaled.reshape(k // 512, 128, 4, n).transpose(0, 1, 3, 2))
    if fmt == "e4m3":
        words = by_word.astype(ml_dtypes.float8_e4m3fn).view(np.uint8)
    else:
        c = by_word.astype(ml_dtypes.float4_e2m1fn).view(np.uint8) & 0xF
        words = c[..., 0::2] | (c[..., 1::2] << 4)
    return np.ascontiguousarray(words), np.ascontiguousarray(byte.astype(np.uint8).reshape(k // 512, 16, n))


def unpack_weight(words, scales, fmt):
    g, p, n, _ = words.shape
    if fmt == "e4m3":
        vals = np.ascontiguousarray(words).view(ml_dtypes.float8_e4m3fn).astype(np.float64)
    else:
        nib = np.empty((g, p, n, 4), np.uint8)
        nib[..., 0::2] = words & 0xF
        nib[..., 1::2] = words >> 4
        vals = E2M1[nib]
    vals = vals * np.repeat(np.exp2(scales.astype(np.float64) - 127.0), 8, axis=1)[..., None]
    return vals.transpose(0, 1, 3, 2).reshape(g * 512, n)

def pack4(w):
    words, scales = pack_weight(w, "e2m1")
    return words.reshape(words.shape[0], 128, -1), scales


def unpack4(words, scales):
    return unpack_weight(words.reshape(words.shape[0], 128, -1, 2), scales, "e2m1")


B, NB, NL, NG, NK = 256, 1024, 1536, 500, 3
N2 = 2 * NB
L2 = 2 * NL


def relu(v):
    return np.maximum(v, 0.0)


def setup_inputs():
    s, t = mx_kscale(N2), mx_kscale(L2)
    Volt = bf(np.random.standard_normal((B, N2)) * s)
    IM = np.random.standard_normal((L2, N2)) / np.sqrt(N2) / s[None, :] * t[:, None]
    Ybr = np.random.standard_normal((L2, L2)) / np.sqrt(L2) / t[None, :]
    L_limit = bf(np.random.random_sample((NL,)) + 0.5)
    n_o_mu_i_u = bf(np.random.standard_normal((B, NL)))
    IM_words, IM_scales = pack4(np.ascontiguousarray(IM.T))
    Ybr_words, Ybr_scales = pack4(np.ascontiguousarray(Ybr.T))
    return {'Volt': Volt,
            'IM_words': IM_words,
            'IM_scales': IM_scales,
            'Ybr_words': Ybr_words,
            'Ybr_scales': Ybr_scales,
            'L_limit': L_limit,
            'n_o_mu_i_u': n_o_mu_i_u}


def reference(Volt, IM_words, IM_scales, Ybr_words, Ybr_scales, L_limit, n_o_mu_i_u):
    d = mxq(f64(Volt), 1, 'e4m3') @ unpack4(IM_words, IM_scales)
    Ibr = mxq(d, 1, 'e4m3') @ unpack4(Ybr_words, Ybr_scales)
    m = Ibr[:, :NL] ** 2 + Ibr[:, NL:] ** 2
    g = m - f64(L_limit) ** 2
    mu = f64(n_o_mu_i_u)
    return relu(g).sum(axis=1) + np.abs(mu * g).sum(axis=1) + relu(-mu).sum(axis=1)

@@ -1,0 +1,286 @@
+from contextlib import ExitStack
+
+import concourse.mybir as mybir
+from concourse.masks import make_identity
+
+F32 = mybir.dt.float32
+BF16 = mybir.dt.bfloat16
+I32 = mybir.dt.int32
+U32 = mybir.dt.uint32
+U8 = mybir.dt.uint8
+FP8X4 = mybir.dt.float8_e4m3fn_x4
+FP4X4 = mybir.dt.float4_e2m1fn_x4
+ALU = mybir.AluOpType
+ACT = mybir.ActivationFunctionType
+
+P = 128
+PACK = 4
+K_GROUP = P * PACK
+N_TILE = 512
+B_TILES = 2
+K1 = 2048
+K2 = 3072
+NL = 1536
+G1 = K1 // K_GROUP
+G2 = K2 // K_GROUP
+HALF_TILES = NL // N_TILE
+FIRST_HALF = range(0, HALF_TILES)
+SECOND_HALF = range(HALF_TILES, 2 * HALF_TILES)
+
+FLOPS = 2 * B_TILES * P * (K1 * K2 + K2 * 2 * NL)
+
+
+def load_scale_planes(nc, planes, scales, groups_per_dma):
+    groups = scales.shape[0]
+    rows = scales.bitcast(I32).rearrange("g q n -> q g n")
+    for g0 in range(0, groups, groups_per_dma):
+        for q in range(8):
+            first = 32 * (q // 4) + q % 4
+            nc.sync.dma_start(
+                out=planes[first:P:64, g0 : g0 + groups_per_dma, :].bitcast(I32),
+                in_=rows[q:16:8, g0 : g0 + groups_per_dma, :],
+            )
+
+
+def load_words(nc, words, dram_words, g, half):
+    int32_cols = slice(half * NL // 2, (half + 1) * NL // 2)
+    byte_cols = slice(half * NL * 2, (half + 1) * NL * 2)
+    nc.sync.dma_start(
+        out=words[:, g, byte_cols].bitcast(I32),
+        in_=dram_words.bitcast(I32)[g, :, int32_cols],
+    )
+
+
+def copy_out(nc, b, out, in_):
+    if b == 0:
+        nc.vector.tensor_copy(out=out, in_=in_)
+    else:
+        nc.scalar.copy(out=out, in_=in_)
+
+
+def mx_pass(nc, acc, codes, code_scales, words, planes, g, b, n):
+    groups = words.shape[1]
+    nc.tensor.matmul_mx(
+        out=acc[:],
+        lhsT=codes[:, g, b, :].bitcast(FP8X4),
+        lhsT_scale=code_scales[:, g, b, :],
+        rhs=words[:, g, 2 * N_TILE * n : 2 * N_TILE * (n + 1)].bitcast(FP4X4),
+        rhs_scale=planes[:, g, N_TILE * n : N_TILE * (n + 1)],
+        start=(g == 0),
+        stop=(g == groups - 1),
+    )
+
+
+def tile_kktloss_pa_kernel(
+    tc, Volt, IM_words, IM_scales, Ybr_words, Ybr_scales, L_limit, n_o_mu_i_u, out
+):
+    nc = tc.nc
+    with ExitStack() as ctx:
+        keep = ctx.enter_context(tc.tile_pool(name="keep", bufs=1))
+        work = ctx.enter_context(tc.tile_pool(name="work", bufs=3))
+        acc_pool = ctx.enter_context(tc.psum_pool(name="acc", bufs=6))
+        turn_pool = ctx.enter_context(tc.psum_pool(name="turn", bufs=2))
+        ctx.enter_context(tc.manual_schedule())
+
+        volt_sb = keep.tile([P, B_TILES, K1], BF16)
+        volt_grouped = keep.tile([P, G1, B_TILES, P, PACK], BF16, align_bytes=64)
+        volt_codes = keep.tile([P, G1, B_TILES, P], U32, align_bytes=64)
+        volt_scales = keep.tile([P, G1, B_TILES, P], U8, align_bytes=64)
+        im_words = keep.tile([P, G1, 2 * K2], U8, align_bytes=64)
+        im_planes = keep.tile([P, G1, K2], U8, align_bytes=64)
+        ybr_words = keep.tile([P, G2, 4 * NL], U8, align_bytes=64)
+        ybr_planes = keep.tile([P, G2, 2 * NL], U8, align_bytes=64)
+        d_sorted = keep.tile([P, G2, B_TILES, PACK, P], BF16)
+        d_grouped = keep.tile([P, G2, B_TILES, P, PACK], BF16, align_bytes=64)
+        d_codes = keep.tile([P, G2, B_TILES, P], U32, align_bytes=64)
+        d_scales = keep.tile([P, G2, B_TILES, P], U8, align_bytes=64)
+        limit_rows = keep.tile([P, NL], BF16)
+        limit_sq = keep.tile([P, NL], F32)
+        mu_sb = keep.tile([P, B_TILES, NL], BF16)
+        abs_mu = keep.tile([P, B_TILES, NL], BF16)
+        min_mu = keep.tile([P, NL], BF16)
+        excess = keep.tile([P, B_TILES, NL], F32)
+        ones = keep.tile([P, P], BF16)
+        ident_f32 = keep.tile([P, P], F32)
+        ident_bf16 = keep.tile([P, P], BF16)
+        g_sums = keep.tile([P, B_TILES, HALF_TILES], F32)
+        abs_sums = keep.tile([P, B_TILES, HALF_TILES], F32)
+        min_mu_sums = keep.tile([P, B_TILES], F32)
+        g_total = keep.tile([P, B_TILES], F32)
+        abs_total = keep.tile([P, B_TILES], F32)
+        loss = keep.tile([P, B_TILES], F32)
+        loss_cols = keep.tile([P, P], F32)
+        loss_rows = keep.tile([P, P], F32)
+
+        make_identity(nc, ident_f32[:])
+        make_identity(nc, ident_bf16[:])
+        nc.vector.memset(limit_rows[:], 0.0)
+        nc.vector.memset(ones[:], 1.0)
+        nc.vector.memset(im_planes[:].rearrange("p g n -> p (g n)").bitcast(I32), 0)
+        nc.vector.memset(ybr_planes[:].rearrange("p g n -> p (g n)").bitcast(I32), 0)
+        nc.vector.memset(loss_cols[:], 0.0)
+
+        nc.sync.dma_start(out=volt_sb[:], in_=Volt.rearrange("(b p) k -> p b k", p=P))
+        nc.sync.dma_start(out=limit_rows[0:1, :], in_=L_limit.rearrange("(o l) -> o l", o=1))
+        load_scale_planes(nc, im_planes, IM_scales, groups_per_dma=2)
+        for half in range(2):
+            for g in range(G1):
+                load_words(nc, im_words, IM_words, g, half)
+        nc.sync.dma_start(out=mu_sb[:], in_=n_o_mu_i_u.rearrange("(b p) l -> p b l", p=P))
+        load_scale_planes(nc, ybr_planes, Ybr_scales, groups_per_dma=3)
+        for half in range(2):
+            for g in range(G2):
+                load_words(nc, ybr_words, Ybr_words, g, half)
+
+        volt_as_words = volt_sb[:].bitcast(F32)
+
+        def quantise_volt(g):
+            nc.vector.quantize_mx(
+                out=volt_codes[:, g].rearrange("p b r -> p (b r)").bitcast(FP8X4),
+                scales=volt_scales[:, g].rearrange("p b r -> p (b r)"),
+                in_=volt_grouped[:, g].rearrange("p b r t -> p (b r t)"),
+            )
+
+        for g in range(G1):
+            for b in range(B_TILES):
+                volt_turned = acc_pool.tile([P, 2, P], F32, name="volt_turned", tag="acc")
+                for u in range(2):
+                    nc.tensor.transpose(
+                        volt_turned[:, u, :],
+                        volt_as_words[:, b, 256 * g + u : 256 * (g + 1) : 2],
+                        ident_f32[:],
+                    )
+                copy_out(
+                    nc,
+                    b,
+                    out=volt_grouped[:, g, b].bitcast(F32),
+                    in_=volt_turned[:].rearrange("p u r -> p r u"),
+                )
+            if g > 0:
+                quantise_volt(g - 1)
+        quantise_volt(G1 - 1)
+
+        for n in FIRST_HALF:
+            cols = slice(N_TILE * n, N_TILE * (n + 1))
+            spread = turn_pool.tile([P, N_TILE], F32, name="spread", tag="turn")
+            nc.tensor.matmul(out=spread[:], lhsT=ones[:], rhs=limit_rows[:, cols], start=True, stop=True)
+            nc.scalar.activation(out=limit_sq[:, cols], in_=spread[:], func=ACT.Square)
+
+        def sort_d(n, b, acc):
+            copy_out(nc, b, out=d_sorted[:, n, b], in_=acc[:].rearrange("r (p t) -> r t p", t=PACK))
+
+        def turn_and_quantise_d(n):
+            for b in range(B_TILES):
+                d_turned = turn_pool.tile([P, PACK, P], BF16, name="d_turned", tag="turn")
+                for t in range(PACK):
+                    nc.tensor.transpose(d_turned[:, t, :], d_sorted[:, n, b, t, :], ident_bf16[:])
+                copy_out(nc, b, out=d_grouped[:, n, b], in_=d_turned[:].rearrange("p t r -> p r t"))
+            nc.vector.quantize_mx(
+                out=d_codes[:, n].rearrange("p b r -> p (b r)").bitcast(FP8X4),
+                scales=d_scales[:, n].rearrange("p b r -> p (b r)"),
+                in_=d_grouped[:, n].rearrange("p b r t -> p (b r t)"),
+            )
+
+        def open_banks(n_tiles):
+            banks = {}
+            for n in n_tiles:
+                for b in range(B_TILES):
+                    banks[(n, b)] = acc_pool.tile([P, N_TILE], F32, name="acc", tag="acc")
+            return banks
+
+        acc = open_banks(FIRST_HALF)
+        for g in range(G1):
+            for n in FIRST_HALF:
+                for b in range(B_TILES):
+                    mx_pass(nc, acc[(n, b)], volt_codes, volt_scales, im_words, im_planes, g, b, n)
+        for n in FIRST_HALF:
+            for b in range(B_TILES):
+                sort_d(n, b, acc[(n, b)])
+        for n in SECOND_HALF:
+            acc = open_banks([n])
+            for b in range(B_TILES):
+                for g in range(G1):
+                    mx_pass(nc, acc[(n, b)], volt_codes, volt_scales, im_words, im_planes, g, b, n)
+                sort_d(n, b, acc[(n, b)])
+            turn_and_quantise_d(n - HALF_TILES)
+
+        acc = open_banks(FIRST_HALF)
+        for g in range(G2):
+            for n in FIRST_HALF:
+                for b in range(B_TILES):
+                    mx_pass(nc, acc[(n, b)], d_codes, d_scales, ybr_words, ybr_planes, g, b, n)
+            if g < HALF_TILES:
+                turn_and_quantise_d(HALF_TILES + g)
+
+        for b in range(B_TILES):
+            nc.scalar.activation(out=abs_mu[:, b, :], in_=mu_sb[:, b, :], func=ACT.Abs)
+            nc.vector.tensor_scalar(
+                out=min_mu[:],
+                in0=mu_sb[:, b, :],
+                scalar1=0.0,
+                scalar2=None,
+                op0=ALU.min,
+                op1=ALU.add,
+                accum_out=min_mu_sums[:, b : b + 1],
+            )
+
+        for n in FIRST_HALF:
+            cols = slice(N_TILE * n, N_TILE * (n + 1))
+            for b in range(B_TILES):
+                nc.scalar.activation(out=excess[:, b, cols], in_=acc[(n, b)][:], func=ACT.Square)
+                nc.vector.tensor_tensor(
+                    out=excess[:, b, cols], in0=excess[:, b, cols], in1=limit_sq[:, cols], op=ALU.subtract
+                )
+
+        def add_absolute(weighted, j, b):
+            absolute = work.tile([P, N_TILE], F32, name="absolute")
+            nc.scalar.activation(
+                out=absolute[:], in_=weighted[:], func=ACT.Abs, accum_out=abs_sums[:, b, j : j + 1]
+            )
+
+        waiting = None
+        for n in SECOND_HALF:
+            j = n - HALF_TILES
+            cols = slice(N_TILE * j, N_TILE * (j + 1))
+            acc = open_banks([n])
+            for b in range(B_TILES):
+                for g in range(G2):
+                    mx_pass(nc, acc[(n, b)], d_codes, d_scales, ybr_words, ybr_planes, g, b, n)
+                im_sq = work.tile([P, N_TILE], F32, name="im_sq")
+                nc.scalar.activation(out=im_sq[:], in_=acc[(n, b)][:], func=ACT.Square)
+                g_tile = work.tile([P, N_TILE], F32, name="g_tile")
+                nc.vector.scalar_tensor_tensor(
+                    out=g_tile[:],
+                    in0=im_sq[:],
+                    scalar=0.0,
+                    in1=excess[:, b, cols],
+                    op0=ALU.add,
+                    op1=ALU.add,
+                    accum_out=g_sums[:, b, j : j + 1],
+                )
+                weighted = work.tile([P, N_TILE], F32, name="weighted")
+                nc.vector.scalar_tensor_tensor(
+                    out=weighted[:],
+                    in0=abs_mu[:, b, cols],
+                    scalar=0.5,
+                    in1=g_tile[:],
+                    op0=ALU.add,
+                    op1=ALU.mult,
+                )
+                if waiting is not None:
+                    add_absolute(*waiting)
+                waiting = (weighted, j, b)
+        add_absolute(*waiting)
+
+        nc.vector.tensor_reduce(out=g_total[:], in_=g_sums[:], axis=mybir.AxisListType.X, op=ALU.add)
+        nc.vector.tensor_reduce(out=abs_total[:], in_=abs_sums[:], axis=mybir.AxisListType.X, op=ALU.add)
+        nc.vector.scalar_tensor_tensor(
+            out=loss[:], in0=g_total[:], scalar=0.5, in1=abs_total[:], op0=ALU.mult, op1=ALU.add
+        )
+        nc.vector.tensor_tensor(
+            out=loss_cols[:, 0:B_TILES], in0=loss[:], in1=min_mu_sums[:], op=ALU.subtract
+        )
+        loss_turned = turn_pool.tile([P, P], F32, name="loss_turned", tag="turn")
+        nc.tensor.transpose(loss_turned[:], loss_cols[:], ident_f32[:])
+        nc.vector.tensor_copy(out=loss_rows[:], in_=loss_turned[:])
+        nc.sync.dma_start(out=out.rearrange("(b r) -> b r", b=B_TILES), in_=loss_rows[0:B_TILES, :])

@@ -112,13 +112,12 @@ def tile_kktloss_pa_kernel(
         loss_cols = keep.tile([P, P], F32)
         loss_rows = keep.tile([P, P], F32)
 
+        nc.vector.memset(im_planes[:].rearrange("p g n -> p (g n)").bitcast(I32), 0)
+        nc.vector.memset(ones[:], 1.0)
+        nc.gpsimd.memset(limit_rows[:].bitcast(I32), 0)
         make_identity(nc, ident_f32[:])
         make_identity(nc, ident_bf16[:])
-        nc.vector.memset(limit_rows[:], 0.0)
-        nc.vector.memset(ones[:], 1.0)
-        nc.vector.memset(im_planes[:].rearrange("p g n -> p (g n)").bitcast(I32), 0)
-        nc.vector.memset(ybr_planes[:].rearrange("p g n -> p (g n)").bitcast(I32), 0)
-        nc.vector.memset(loss_cols[:], 0.0)
+        nc.gpsimd.memset(loss_cols[:], 0.0)
 
         nc.sync.dma_start(out=volt_sb[:], in_=Volt.rearrange("(b p) k -> p b k", p=P))
         nc.sync.dma_start(out=limit_rows[0:1, :], in_=L_limit.rearrange("(o l) -> o l", o=1))
@@ -127,11 +126,6 @@ def tile_kktloss_pa_kernel(
             for g in range(G1):
                 load_words(nc, im_words, IM_words, g, half)
         nc.sync.dma_start(out=mu_sb[:], in_=n_o_mu_i_u.rearrange("(b p) l -> p b l", p=P))
-        load_scale_planes(nc, ybr_planes, Ybr_scales, groups_per_dma=3)
-        for half in range(2):
-            for g in range(G2):
-                load_words(nc, ybr_words, Ybr_words, g, half)
-
         volt_as_words = volt_sb[:].bitcast(F32)
 
         def quantise_volt(g):
@@ -159,6 +153,12 @@ def tile_kktloss_pa_kernel(
             if g > 0:
                 quantise_volt(g - 1)
         quantise_volt(G1 - 1)
+        nc.vector.memset(ybr_planes[:].rearrange("p g n -> p (g n)").bitcast(I32), 0)
+
+        load_scale_planes(nc, ybr_planes, Ybr_scales, groups_per_dma=3)
+        for half in range(2):
+            for g in range(G2):
+                load_words(nc, ybr_words, Ybr_words, g, half)
 
         for n in FIRST_HALF:
             cols = slice(N_TILE * n, N_TILE * (n + 1))

@@ -30,14 +30,15 @@ SECOND_HALF = range(HALF_TILES, 2 * HALF_TILES)
 FLOPS = 2 * B_TILES * P * (K1 * K2 + K2 * 2 * NL)
 
 
-def load_scale_planes(nc, planes, scales, groups_per_dma):
+def load_scale_planes(nc, planes, scales, groups_per_dma, half=None):
     groups = scales.shape[0]
-    rows = scales.bitcast(I32).rearrange("g q n -> q g n")
+    first_col, last_col = (0, 2 * NL) if half is None else (half * NL, (half + 1) * NL)
+    rows = scales.bitcast(I32).rearrange("g q n -> q g n")[:, :, first_col // 4 : last_col // 4]
     for g0 in range(0, groups, groups_per_dma):
         for q in range(8):
             first = 32 * (q // 4) + q % 4
             nc.sync.dma_start(
-                out=planes[first:P:64, g0 : g0 + groups_per_dma, :].bitcast(I32),
+                out=planes[first:P:64, g0 : g0 + groups_per_dma, first_col:last_col].bitcast(I32),
                 in_=rows[q:16:8, g0 : g0 + groups_per_dma, :],
             )
 
@@ -121,8 +122,8 @@ def tile_kktloss_pa_kernel(
 
         nc.sync.dma_start(out=volt_sb[:], in_=Volt.rearrange("(b p) k -> p b k", p=P))
         nc.sync.dma_start(out=limit_rows[0:1, :], in_=L_limit.rearrange("(o l) -> o l", o=1))
-        load_scale_planes(nc, im_planes, IM_scales, groups_per_dma=2)
         for half in range(2):
+            load_scale_planes(nc, im_planes, IM_scales, groups_per_dma=G1, half=half)
             for g in range(G1):
                 load_words(nc, im_words, IM_words, g, half)
         nc.sync.dma_start(out=mu_sb[:], in_=n_o_mu_i_u.rearrange("(b p) l -> p b l", p=P))

@@ -30,15 +30,15 @@ SECOND_HALF = range(HALF_TILES, 2 * HALF_TILES)
 FLOPS = 2 * B_TILES * P * (K1 * K2 + K2 * 2 * NL)
 
 
-def load_scale_planes(nc, planes, scales, groups_per_dma, half=None):
+def load_scale_planes(nc, planes, scales, half, groups_per_dma):
     groups = scales.shape[0]
-    first_col, last_col = (0, 2 * NL) if half is None else (half * NL, (half + 1) * NL)
-    rows = scales.bitcast(I32).rearrange("g q n -> q g n")[:, :, first_col // 4 : last_col // 4]
+    int32_cols = slice(half * NL // 4, (half + 1) * NL // 4)
+    rows = scales.bitcast(I32).rearrange("g q n -> q g n")[:, :, int32_cols]
     for g0 in range(0, groups, groups_per_dma):
         for q in range(8):
             first = 32 * (q // 4) + q % 4
             nc.sync.dma_start(
-                out=planes[first:P:64, g0 : g0 + groups_per_dma, first_col:last_col].bitcast(I32),
+                out=planes[first:P:64, g0 : g0 + groups_per_dma, :].bitcast(I32),
                 in_=rows[q:16:8, g0 : g0 + groups_per_dma, :],
             )
 
@@ -66,7 +66,7 @@ def mx_pass(nc, acc, codes, code_scales, words, planes, g, b, n):
         lhsT=codes[:, g, b, :].bitcast(FP8X4),
         lhsT_scale=code_scales[:, g, b, :],
         rhs=words[:, g, 2 * N_TILE * n : 2 * N_TILE * (n + 1)].bitcast(FP4X4),
-        rhs_scale=planes[:, g, N_TILE * n : N_TILE * (n + 1)],
+        rhs_scale=planes[n // HALF_TILES][:, g, N_TILE * (n % HALF_TILES) : N_TILE * (n % HALF_TILES + 1)],
         start=(g == 0),
         stop=(g == groups - 1),
     )
@@ -88,9 +88,13 @@ def tile_kktloss_pa_kernel(
         volt_codes = keep.tile([P, G1, B_TILES, P], U32, align_bytes=64)
         volt_scales = keep.tile([P, G1, B_TILES, P], U8, align_bytes=64)
         im_words = keep.tile([P, G1, 2 * K2], U8, align_bytes=64)
-        im_planes = keep.tile([P, G1, K2], U8, align_bytes=64)
+        im_planes_0 = keep.tile([P, G1, NL], U8, align_bytes=64)
+        im_planes_1 = keep.tile([P, G1, NL], U8, align_bytes=64)
+        im_planes = [im_planes_0, im_planes_1]
         ybr_words = keep.tile([P, G2, 4 * NL], U8, align_bytes=64)
-        ybr_planes = keep.tile([P, G2, 2 * NL], U8, align_bytes=64)
+        ybr_planes_0 = keep.tile([P, G2, NL], U8, align_bytes=64)
+        ybr_planes_1 = keep.tile([P, G2, NL], U8, align_bytes=64)
+        ybr_planes = [ybr_planes_0, ybr_planes_1]
         d_sorted = keep.tile([P, G2, B_TILES, PACK, P], BF16)
         d_grouped = keep.tile([P, G2, B_TILES, P, PACK], BF16, align_bytes=64)
         d_codes = keep.tile([P, G2, B_TILES, P], U32, align_bytes=64)
@@ -113,7 +117,8 @@ def tile_kktloss_pa_kernel(
         loss_cols = keep.tile([P, P], F32)
         loss_rows = keep.tile([P, P], F32)
 
-        nc.vector.memset(im_planes[:].rearrange("p g n -> p (g n)").bitcast(I32), 0)
+        for planes in im_planes:
+            nc.vector.memset(planes[:].rearrange("p g n -> p (g n)").bitcast(I32), 0)
         nc.vector.memset(ones[:], 1.0)
         nc.gpsimd.memset(limit_rows[:].bitcast(I32), 0)
         make_identity(nc, ident_f32[:])
@@ -123,7 +128,7 @@ def tile_kktloss_pa_kernel(
         nc.sync.dma_start(out=volt_sb[:], in_=Volt.rearrange("(b p) k -> p b k", p=P))
         nc.sync.dma_start(out=limit_rows[0:1, :], in_=L_limit.rearrange("(o l) -> o l", o=1))
         for half in range(2):
-            load_scale_planes(nc, im_planes, IM_scales, groups_per_dma=G1, half=half)
+            load_scale_planes(nc, im_planes[half], IM_scales, half, groups_per_dma=G1)
             for g in range(G1):
                 load_words(nc, im_words, IM_words, g, half)
         nc.sync.dma_start(out=mu_sb[:], in_=n_o_mu_i_u.rearrange("(b p) l -> p b l", p=P))
@@ -154,9 +159,11 @@ def tile_kktloss_pa_kernel(
             if g > 0:
                 quantise_volt(g - 1)
         quantise_volt(G1 - 1)
-        nc.vector.memset(ybr_planes[:].rearrange("p g n -> p (g n)").bitcast(I32), 0)
+        for planes in ybr_planes:
+            nc.vector.memset(planes[:].rearrange("p g n -> p (g n)").bitcast(I32), 0)
 
-        load_scale_planes(nc, ybr_planes, Ybr_scales, groups_per_dma=3)
+        for half in range(2):
+            load_scale_planes(nc, ybr_planes[half], Ybr_scales, half, groups_per_dma=G2)
         for half in range(2):
             for g in range(G2):
                 load_words(nc, ybr_words, Ybr_words, g, half)

@@ -131,7 +131,6 @@ def tile_kktloss_pa_kernel(
             load_scale_planes(nc, im_planes[half], IM_scales, half, groups_per_dma=G1)
             for g in range(G1):
                 load_words(nc, im_words, IM_words, g, half)
-        nc.sync.dma_start(out=mu_sb[:], in_=n_o_mu_i_u.rearrange("(b p) l -> p b l", p=P))
         volt_as_words = volt_sb[:].bitcast(F32)
 
         def quantise_volt(g):
@@ -164,9 +163,10 @@ def tile_kktloss_pa_kernel(
 
         for half in range(2):
             load_scale_planes(nc, ybr_planes[half], Ybr_scales, half, groups_per_dma=G2)
-        for half in range(2):
             for g in range(G2):
                 load_words(nc, ybr_words, Ybr_words, g, half)
+            if half == 0:
+                nc.sync.dma_start(out=mu_sb[:], in_=n_o_mu_i_u.rearrange("(b p) l -> p b l", p=P))
 
         for n in FIRST_HALF:
             cols = slice(N_TILE * n, N_TILE * (n + 1))

@@ -1,3 +1,4 @@
+import math
 from contextlib import ExitStack
 
 import concourse.mybir as mybir
@@ -26,6 +27,10 @@ G2 = K2 // K_GROUP
 HALF_TILES = NL // N_TILE
 FIRST_HALF = range(0, HALF_TILES)
 SECOND_HALF = range(HALF_TILES, 2 * HALF_TILES)
+
+TURN = 32
+TERMS = 9
+SQRT_HALF = math.sqrt(0.5)
 
 FLOPS = 2 * B_TILES * P * (K1 * K2 + K2 * 2 * NL)
 
@@ -59,14 +64,16 @@ def copy_out(nc, b, out, in_):
         nc.scalar.copy(out=out, in_=in_)
 
 
-def mx_pass(nc, acc, codes, code_scales, words, planes, g, b, n):
+def mx_pass(nc, acc, codes, code_scales, words, planes, g, b, first):
     groups = words.shape[1]
+    width = acc.shape[-1]
+    half, col = divmod(first, NL)
     nc.tensor.matmul_mx(
-        out=acc[:],
+        out=acc,
         lhsT=codes[:, g, b, :].bitcast(FP8X4),
         lhsT_scale=code_scales[:, g, b, :],
-        rhs=words[:, g, 2 * N_TILE * n : 2 * N_TILE * (n + 1)].bitcast(FP4X4),
-        rhs_scale=planes[n // HALF_TILES][:, g, N_TILE * (n % HALF_TILES) : N_TILE * (n % HALF_TILES + 1)],
+        rhs=words[:, g, 2 * first : 2 * (first + width)].bitcast(FP4X4),
+        rhs_scale=planes[half][:, g, col : col + width],
         start=(g == 0),
         stop=(g == groups - 1),
     )
@@ -95,7 +102,7 @@ def tile_kktloss_pa_kernel(
         ybr_planes_0 = keep.tile([P, G2, NL], U8, align_bytes=64)
         ybr_planes_1 = keep.tile([P, G2, NL], U8, align_bytes=64)
         ybr_planes = [ybr_planes_0, ybr_planes_1]
-        d_sorted = keep.tile([P, G2, B_TILES, PACK, P], BF16)
+        d_sorted = keep.tile([P, G2, B_TILES, 2, P, 2], BF16)
         d_grouped = keep.tile([P, G2, B_TILES, P, PACK], BF16, align_bytes=64)
         d_codes = keep.tile([P, G2, B_TILES, P], U32, align_bytes=64)
         d_scales = keep.tile([P, G2, B_TILES, P], U8, align_bytes=64)
@@ -103,27 +110,21 @@ def tile_kktloss_pa_kernel(
         limit_sq = keep.tile([P, NL], F32)
         mu_sb = keep.tile([P, B_TILES, NL], BF16)
         abs_mu = keep.tile([P, B_TILES, NL], BF16)
-        min_mu = keep.tile([P, NL], BF16)
+        min_mu = keep.tile([P, NL], F32)
         excess = keep.tile([P, B_TILES, NL], F32)
         ones = keep.tile([P, P], BF16)
         ident_f32 = keep.tile([P, P], F32)
-        ident_bf16 = keep.tile([P, P], BF16)
-        g_sums = keep.tile([P, B_TILES, HALF_TILES], F32)
-        abs_sums = keep.tile([P, B_TILES, HALF_TILES], F32)
-        min_mu_sums = keep.tile([P, B_TILES], F32)
-        g_total = keep.tile([P, B_TILES], F32)
-        abs_total = keep.tile([P, B_TILES], F32)
-        loss = keep.tile([P, B_TILES], F32)
-        loss_cols = keep.tile([P, P], F32)
-        loss_rows = keep.tile([P, P], F32)
+        terms = keep.tile([P, B_TILES, TERMS], F32)
+        loss_cols = keep.tile([P, TURN], F32, align_bytes=64)
+        loss_rows = keep.tile([P, TURN], F32, align_bytes=64)
 
         for planes in im_planes:
             nc.vector.memset(planes[:].rearrange("p g n -> p (g n)").bitcast(I32), 0)
         nc.vector.memset(ones[:], 1.0)
         nc.gpsimd.memset(limit_rows[:].bitcast(I32), 0)
         make_identity(nc, ident_f32[:])
-        make_identity(nc, ident_bf16[:])
         nc.gpsimd.memset(loss_cols[:], 0.0)
+        nc.gpsimd.memset(terms[:], 0.0)
 
         nc.sync.dma_start(out=volt_sb[:], in_=Volt.rearrange("(b p) k -> p b k", p=P))
         nc.sync.dma_start(out=limit_rows[0:1, :], in_=L_limit.rearrange("(o l) -> o l", o=1))
@@ -172,17 +173,26 @@ def tile_kktloss_pa_kernel(
             cols = slice(N_TILE * n, N_TILE * (n + 1))
             spread = turn_pool.tile([P, N_TILE], F32, name="spread", tag="turn")
             nc.tensor.matmul(out=spread[:], lhsT=ones[:], rhs=limit_rows[:, cols], start=True, stop=True)
-            nc.scalar.activation(out=limit_sq[:, cols], in_=spread[:], func=ACT.Square)
+            nc.scalar.activation(out=limit_sq[:, cols], in_=spread[:], func=ACT.Square, scale=SQRT_HALF)
 
         def sort_d(n, b, acc):
-            copy_out(nc, b, out=d_sorted[:, n, b], in_=acc[:].rearrange("r (p t) -> r t p", t=PACK))
+            copy_out(nc, b, out=d_sorted[:, n, b], in_=acc[:].rearrange("r (p u e) -> r u p e", u=2, e=2))
 
         def turn_and_quantise_d(n):
             for b in range(B_TILES):
-                d_turned = turn_pool.tile([P, PACK, P], BF16, name="d_turned", tag="turn")
-                for t in range(PACK):
-                    nc.tensor.transpose(d_turned[:, t, :], d_sorted[:, n, b, t, :], ident_bf16[:])
-                copy_out(nc, b, out=d_grouped[:, n, b], in_=d_turned[:].rearrange("p t r -> p r t"))
+                d_turned = turn_pool.tile([P, 2, P], F32, name="d_turned", tag="turn")
+                for u in range(2):
+                    nc.tensor.transpose(
+                        d_turned[:, u, :],
+                        d_sorted[:, n, b, u].rearrange("r p e -> r (p e)").bitcast(F32),
+                        ident_f32[:],
+                    )
+                copy_out(
+                    nc,
+                    b,
+                    out=d_grouped[:, n, b].bitcast(F32),
+                    in_=d_turned[:].rearrange("p u r -> p r u"),
+                )
             nc.vector.quantize_mx(
                 out=d_codes[:, n].rearrange("p b r -> p (b r)").bitcast(FP8X4),
                 scales=d_scales[:, n].rearrange("p b r -> p (b r)"),
@@ -200,7 +210,7 @@ def tile_kktloss_pa_kernel(
         for g in range(G1):
             for n in FIRST_HALF:
                 for b in range(B_TILES):
-                    mx_pass(nc, acc[(n, b)], volt_codes, volt_scales, im_words, im_planes, g, b, n)
+                    mx_pass(nc, acc[(n, b)][:], volt_codes, volt_scales, im_words, im_planes, g, b, N_TILE * n)
         for n in FIRST_HALF:
             for b in range(B_TILES):
                 sort_d(n, b, acc[(n, b)])
@@ -208,7 +218,7 @@ def tile_kktloss_pa_kernel(
             acc = open_banks([n])
             for b in range(B_TILES):
                 for g in range(G1):
-                    mx_pass(nc, acc[(n, b)], volt_codes, volt_scales, im_words, im_planes, g, b, n)
+                    mx_pass(nc, acc[(n, b)][:], volt_codes, volt_scales, im_words, im_planes, g, b, N_TILE * n)
                 sort_d(n, b, acc[(n, b)])
             turn_and_quantise_d(n - HALF_TILES)
 
@@ -216,7 +226,7 @@ def tile_kktloss_pa_kernel(
         for g in range(G2):
             for n in FIRST_HALF:
                 for b in range(B_TILES):
-                    mx_pass(nc, acc[(n, b)], d_codes, d_scales, ybr_words, ybr_planes, g, b, n)
+                    mx_pass(nc, acc[(n, b)][:], d_codes, d_scales, ybr_words, ybr_planes, g, b, N_TILE * n)
             if g < HALF_TILES:
                 turn_and_quantise_d(HALF_TILES + g)
 
@@ -228,67 +238,90 @@ def tile_kktloss_pa_kernel(
                 scalar1=0.0,
                 scalar2=None,
                 op0=ALU.min,
-                op1=ALU.add,
-                accum_out=min_mu_sums[:, b : b + 1],
+                op1=ALU.subtract,
+                accum_out=terms[:, b, TERMS - 1 : TERMS],
             )
 
         for n in FIRST_HALF:
             cols = slice(N_TILE * n, N_TILE * (n + 1))
             for b in range(B_TILES):
-                nc.scalar.activation(out=excess[:, b, cols], in_=acc[(n, b)][:], func=ACT.Square)
+                nc.scalar.activation(
+                    out=excess[:, b, cols], in_=acc[(n, b)][:], func=ACT.Square, scale=SQRT_HALF
+                )
                 nc.vector.tensor_tensor(
                     out=excess[:, b, cols], in0=excess[:, b, cols], in1=limit_sq[:, cols], op=ALU.subtract
                 )
 
-        def add_absolute(weighted, j, b):
+        def add_absolute(weighted, width, b, term):
             absolute = work.tile([P, N_TILE], F32, name="absolute")
             nc.scalar.activation(
-                out=absolute[:], in_=weighted[:], func=ACT.Abs, accum_out=abs_sums[:, b, j : j + 1]
+                out=absolute[:, 0:width],
+                in_=weighted[:, 0:width],
+                func=ACT.Abs,
+                scale=2.0,
+                accum_out=terms[:, b, term : term + 1],
             )
 
+        def pieces(n, b):
+            first = N_TILE * (n - HALF_TILES)
+            if (n, b) == (SECOND_HALF[-1], B_TILES - 1):
+                return [(first, N_TILE // 2, P), (first + N_TILE // 2, N_TILE // 2, P)]
+            return [(first, N_TILE, N_TILE)]
+
+        next_term = [0] * B_TILES
         waiting = None
         for n in SECOND_HALF:
-            j = n - HALF_TILES
-            cols = slice(N_TILE * j, N_TILE * (j + 1))
-            acc = open_banks([n])
             for b in range(B_TILES):
-                for g in range(G2):
-                    mx_pass(nc, acc[(n, b)], d_codes, d_scales, ybr_words, ybr_planes, g, b, n)
-                im_sq = work.tile([P, N_TILE], F32, name="im_sq")
-                nc.scalar.activation(out=im_sq[:], in_=acc[(n, b)][:], func=ACT.Square)
-                g_tile = work.tile([P, N_TILE], F32, name="g_tile")
-                nc.vector.scalar_tensor_tensor(
-                    out=g_tile[:],
-                    in0=im_sq[:],
-                    scalar=0.0,
-                    in1=excess[:, b, cols],
-                    op0=ALU.add,
-                    op1=ALU.add,
-                    accum_out=g_sums[:, b, j : j + 1],
-                )
-                weighted = work.tile([P, N_TILE], F32, name="weighted")
-                nc.vector.scalar_tensor_tensor(
-                    out=weighted[:],
-                    in0=abs_mu[:, b, cols],
-                    scalar=0.5,
-                    in1=g_tile[:],
-                    op0=ALU.add,
-                    op1=ALU.mult,
-                )
-                if waiting is not None:
-                    add_absolute(*waiting)
-                waiting = (weighted, j, b)
+                for first, width, pass_width in pieces(n, b):
+                    cols = slice(first, first + width)
+                    acc = acc_pool.tile([P, N_TILE], F32, name="acc", tag="acc")
+                    for col in range(0, width, pass_width):
+                        for g in range(G2):
+                            mx_pass(
+                                nc,
+                                acc[:, col : col + pass_width],
+                                d_codes,
+                                d_scales,
+                                ybr_words,
+                                ybr_planes,
+                                g,
+                                b,
+                                NL + first + col,
+                            )
+                    term = next_term[b]
+                    next_term[b] += 2
+                    im_sq = work.tile([P, N_TILE], F32, name="im_sq")
+                    nc.scalar.activation(
+                        out=im_sq[:, 0:width], in_=acc[:, 0:width], func=ACT.Square, scale=SQRT_HALF
+                    )
+                    h_tile = work.tile([P, N_TILE], F32, name="h_tile")
+                    nc.vector.scalar_tensor_tensor(
+                        out=h_tile[:, 0:width],
+                        in0=im_sq[:, 0:width],
+                        scalar=0.0,
+                        in1=excess[:, b, cols],
+                        op0=ALU.add,
+                        op1=ALU.add,
+                        accum_out=terms[:, b, term : term + 1],
+                    )
+                    weighted = work.tile([P, N_TILE], F32, name="weighted")
+                    nc.vector.scalar_tensor_tensor(
+                        out=weighted[:, 0:width],
+                        in0=abs_mu[:, b, cols],
+                        scalar=0.5,
+                        in1=h_tile[:, 0:width],
+                        op0=ALU.add,
+                        op1=ALU.mult,
+                    )
+                    if waiting is not None:
+                        add_absolute(*waiting)
+                    waiting = (weighted, width, b, term + 1)
         add_absolute(*waiting)
 
-        nc.vector.tensor_reduce(out=g_total[:], in_=g_sums[:], axis=mybir.AxisListType.X, op=ALU.add)
-        nc.vector.tensor_reduce(out=abs_total[:], in_=abs_sums[:], axis=mybir.AxisListType.X, op=ALU.add)
-        nc.vector.scalar_tensor_tensor(
-            out=loss[:], in0=g_total[:], scalar=0.5, in1=abs_total[:], op0=ALU.mult, op1=ALU.add
+        nc.vector.tensor_reduce(
+            out=loss_cols[:, 0:B_TILES], in_=terms[:], axis=mybir.AxisListType.X, op=ALU.add
         )
-        nc.vector.tensor_tensor(
-            out=loss_cols[:, 0:B_TILES], in0=loss[:], in1=min_mu_sums[:], op=ALU.subtract
-        )
-        loss_turned = turn_pool.tile([P, P], F32, name="loss_turned", tag="turn")
-        nc.tensor.transpose(loss_turned[:], loss_cols[:], ident_f32[:])
-        nc.vector.tensor_copy(out=loss_rows[:], in_=loss_turned[:])
-        nc.sync.dma_start(out=out.rearrange("(b r) -> b r", b=B_TILES), in_=loss_rows[0:B_TILES, :])
+        nc.vector.transpose(out=loss_rows[:], in_=loss_cols[:])
+        out_runs = out.rearrange("(b q r) -> b q r", b=B_TILES, r=TURN)
+        for b in range(B_TILES):
+            nc.sync.dma_start(out=out_runs[b], in_=loss_rows[b:P:TURN, :])

@@ -28,6 +28,7 @@ HALF_TILES = NL // N_TILE
 FIRST_HALF = range(0, HALF_TILES)
 SECOND_HALF = range(HALF_TILES, 2 * HALF_TILES)
 
+WARM_UP = 8
 TURN = 32
 TERMS = 9
 SQRT_HALF = math.sqrt(0.5)
@@ -112,15 +113,15 @@ def tile_kktloss_pa_kernel(
         abs_mu = keep.tile([P, B_TILES, NL], BF16)
         min_mu = keep.tile([P, NL], F32)
         excess = keep.tile([P, B_TILES, NL], F32)
-        ones = keep.tile([P, P], BF16)
+        ones = keep.tile([P, N_TILE], BF16)
         ident_f32 = keep.tile([P, P], F32)
         terms = keep.tile([P, B_TILES, TERMS], F32)
         loss_cols = keep.tile([P, TURN], F32, align_bytes=64)
         loss_rows = keep.tile([P, TURN], F32, align_bytes=64)
 
+        nc.vector.memset(ones[:], 1.0)
         for planes in im_planes:
             nc.vector.memset(planes[:].rearrange("p g n -> p (g n)").bitcast(I32), 0)
-        nc.vector.memset(ones[:], 1.0)
         nc.gpsimd.memset(limit_rows[:].bitcast(I32), 0)
         make_identity(nc, ident_f32[:])
         nc.gpsimd.memset(loss_cols[:], 0.0)
@@ -132,6 +133,17 @@ def tile_kktloss_pa_kernel(
             load_scale_planes(nc, im_planes[half], IM_scales, half, groups_per_dma=G1)
             for g in range(G1):
                 load_words(nc, im_words, IM_words, g, half)
+
+        for i in range(WARM_UP):
+            warm = turn_pool.tile([P, N_TILE], F32, name="warm", tag="turn")
+            nc.tensor.matmul(out=warm[:], lhsT=ones[:, 0:P], rhs=ones[:], start=True, stop=True)
+
+        def spread_limit(n):
+            cols = slice(N_TILE * n, N_TILE * (n + 1))
+            spread = turn_pool.tile([P, N_TILE], F32, name="spread", tag="turn")
+            nc.tensor.matmul(out=spread[:], lhsT=ones[:, 0:P], rhs=limit_rows[:, cols], start=True, stop=True)
+            nc.scalar.activation(out=limit_sq[:, cols], in_=spread[:], func=ACT.Square, scale=SQRT_HALF)
+
         volt_as_words = volt_sb[:].bitcast(F32)
 
         def quantise_volt(g):
@@ -158,6 +170,8 @@ def tile_kktloss_pa_kernel(
                 )
             if g > 0:
                 quantise_volt(g - 1)
+            if g in FIRST_HALF:
+                spread_limit(g)
         quantise_volt(G1 - 1)
         for planes in ybr_planes:
             nc.vector.memset(planes[:].rearrange("p g n -> p (g n)").bitcast(I32), 0)
@@ -168,12 +182,6 @@ def tile_kktloss_pa_kernel(
                 load_words(nc, ybr_words, Ybr_words, g, half)
             if half == 0:
                 nc.sync.dma_start(out=mu_sb[:], in_=n_o_mu_i_u.rearrange("(b p) l -> p b l", p=P))
-
-        for n in FIRST_HALF:
-            cols = slice(N_TILE * n, N_TILE * (n + 1))
-            spread = turn_pool.tile([P, N_TILE], F32, name="spread", tag="turn")
-            nc.tensor.matmul(out=spread[:], lhsT=ones[:], rhs=limit_rows[:, cols], start=True, stop=True)
-            nc.scalar.activation(out=limit_sq[:, cols], in_=spread[:], func=ACT.Square, scale=SQRT_HALF)
 
         def sort_d(n, b, acc):
             copy_out(nc, b, out=d_sorted[:, n, b], in_=acc[:].rearrange("r (p u e) -> r u p e", u=2, e=2))

@@ -58,6 +58,14 @@ def load_words(nc, words, dram_words, g, half):
     )
 
 
+def load_column_tile(nc, words, dram_words, n):
+    int32_cols = slice(n * N_TILE // 2, (n + 1) * N_TILE // 2)
+    nc.sync.dma_start(
+        out=words[:].bitcast(I32),
+        in_=dram_words.bitcast(I32)[:, :, int32_cols].rearrange("g p c -> p g c"),
+    )
+
+
 def copy_out(nc, b, out, in_):
     if b == 0:
         nc.vector.tensor_copy(out=out, in_=in_)
@@ -66,14 +74,15 @@ def copy_out(nc, b, out, in_):
 
 
 def mx_pass(nc, acc, codes, code_scales, words, planes, g, b, first):
-    groups = words.shape[1]
-    width = acc.shape[-1]
     half, col = divmod(first, NL)
+    width = acc.shape[-1]
+    tile, tile_first = words(first)
+    groups = tile.shape[1]
     nc.tensor.matmul_mx(
         out=acc,
         lhsT=codes[:, g, b, :].bitcast(FP8X4),
         lhsT_scale=code_scales[:, g, b, :],
-        rhs=words[:, g, 2 * first : 2 * (first + width)].bitcast(FP4X4),
+        rhs=tile[:, g, 2 * (first - tile_first) : 2 * (first - tile_first + width)].bitcast(FP4X4),
         rhs_scale=planes[half][:, g, col : col + width],
         start=(g == 0),
         stop=(g == groups - 1),
@@ -95,11 +104,26 @@ def tile_kktloss_pa_kernel(
         volt_grouped = keep.tile([P, G1, B_TILES, P, PACK], BF16, align_bytes=64)
         volt_codes = keep.tile([P, G1, B_TILES, P], U32, align_bytes=64)
         volt_scales = keep.tile([P, G1, B_TILES, P], U8, align_bytes=64)
-        im_words = keep.tile([P, G1, 2 * K2], U8, align_bytes=64)
+        im_tile = keep.tile([P, G1, 2 * K2], U8, align_bytes=64)
+
+        def im_words(first):
+            return im_tile, 0
+
         im_planes_0 = keep.tile([P, G1, NL], U8, align_bytes=64)
         im_planes_1 = keep.tile([P, G1, NL], U8, align_bytes=64)
         im_planes = [im_planes_0, im_planes_1]
-        ybr_words = keep.tile([P, G2, 4 * NL], U8, align_bytes=64)
+        ybr_half = keep.tile([P, G2, 2 * NL], U8, align_bytes=64)
+        ybr_tile_3 = keep.tile([P, G2, 2 * N_TILE], U8, align_bytes=64)
+        ybr_tile_4 = keep.tile([P, G2, 2 * N_TILE], U8, align_bytes=64)
+        ybr_tile_5 = keep.tile([P, G2, 2 * N_TILE], U8, align_bytes=64)
+        ybr_tiles = {3: ybr_tile_3, 4: ybr_tile_4, 5: ybr_tile_5}
+
+        def ybr_words(first):
+            n = first // N_TILE
+            if n in SECOND_HALF:
+                return ybr_tiles[n], N_TILE * n
+            return ybr_half, 0
+
         ybr_planes_0 = keep.tile([P, G2, NL], U8, align_bytes=64)
         ybr_planes_1 = keep.tile([P, G2, NL], U8, align_bytes=64)
         ybr_planes = [ybr_planes_0, ybr_planes_1]
@@ -132,7 +156,7 @@ def tile_kktloss_pa_kernel(
         for half in range(2):
             load_scale_planes(nc, im_planes[half], IM_scales, half, groups_per_dma=G1)
             for g in range(G1):
-                load_words(nc, im_words, IM_words, g, half)
+                load_words(nc, im_tile, IM_words, g, half)
 
         for i in range(WARM_UP):
             warm = turn_pool.tile([P, N_TILE], F32, name="warm", tag="turn")
@@ -176,12 +200,13 @@ def tile_kktloss_pa_kernel(
         for planes in ybr_planes:
             nc.vector.memset(planes[:].rearrange("p g n -> p (g n)").bitcast(I32), 0)
 
-        for half in range(2):
-            load_scale_planes(nc, ybr_planes[half], Ybr_scales, half, groups_per_dma=G2)
-            for g in range(G2):
-                load_words(nc, ybr_words, Ybr_words, g, half)
-            if half == 0:
-                nc.sync.dma_start(out=mu_sb[:], in_=n_o_mu_i_u.rearrange("(b p) l -> p b l", p=P))
+        load_scale_planes(nc, ybr_planes[0], Ybr_scales, 0, groups_per_dma=G2)
+        for g in range(G2):
+            load_words(nc, ybr_half, Ybr_words, g, 0)
+        nc.sync.dma_start(out=mu_sb[:], in_=n_o_mu_i_u.rearrange("(b p) l -> p b l", p=P))
+        load_scale_planes(nc, ybr_planes[1], Ybr_scales, 1, groups_per_dma=G2)
+        for n in SECOND_HALF:
+            load_column_tile(nc, ybr_tiles[n], Ybr_words, n)
 
         def sort_d(n, b, acc):
             copy_out(nc, b, out=d_sorted[:, n, b], in_=acc[:].rearrange("r (p u e) -> r u p e", u=2, e=2))
@@ -222,13 +247,22 @@ def tile_kktloss_pa_kernel(
         for n in FIRST_HALF:
             for b in range(B_TILES):
                 sort_d(n, b, acc[(n, b)])
-        for n in SECOND_HALF:
-            acc = open_banks([n])
-            for b in range(B_TILES):
-                for g in range(G1):
+        acc = open_banks(SECOND_HALF[0:2])
+        for g in range(G1):
+            for n in SECOND_HALF[0:2]:
+                for b in range(B_TILES):
                     mx_pass(nc, acc[(n, b)][:], volt_codes, volt_scales, im_words, im_planes, g, b, N_TILE * n)
+            if g < HALF_TILES:
+                turn_and_quantise_d(g)
+        for n in SECOND_HALF[0:2]:
+            for b in range(B_TILES):
                 sort_d(n, b, acc[(n, b)])
-            turn_and_quantise_d(n - HALF_TILES)
+        n = SECOND_HALF[2]
+        acc = open_banks([n])
+        for b in range(B_TILES):
+            for g in range(G1):
+                mx_pass(nc, acc[(n, b)][:], volt_codes, volt_scales, im_words, im_planes, g, b, N_TILE * n)
+            sort_d(n, b, acc[(n, b)])
 
         acc = open_banks(FIRST_HALF)
         for g in range(G2):
@@ -277,7 +311,7 @@ def tile_kktloss_pa_kernel(
             return [(first, N_TILE, N_TILE)]
 
         next_term = [0] * B_TILES
-        waiting = None
+        waiting = []
         for n in SECOND_HALF:
             for b in range(B_TILES):
                 for first, width, pass_width in pieces(n, b):
@@ -321,10 +355,11 @@ def tile_kktloss_pa_kernel(
                         op0=ALU.add,
                         op1=ALU.mult,
                     )
-                    if waiting is not None:
-                        add_absolute(*waiting)
-                    waiting = (weighted, width, b, term + 1)
-        add_absolute(*waiting)
+                    waiting.append((weighted, width, b, term + 1))
+                    if len(waiting) > 2:
+                        add_absolute(*waiting.pop(0))
+        for piece in waiting:
+            add_absolute(*piece)
 
         nc.vector.tensor_reduce(
             out=loss_cols[:, 0:B_TILES], in_=terms[:], axis=mybir.AxisListType.X, op=ALU.add

@@ -30,7 +30,7 @@ SECOND_HALF = range(HALF_TILES, 2 * HALF_TILES)
 
 WARM_UP = 8
 TURN = 32
-TERMS = 9
+TERMS = 12
 SQRT_HALF = math.sqrt(0.5)
 
 FLOPS = 2 * B_TILES * P * (K1 * K2 + K2 * 2 * NL)
@@ -58,16 +58,20 @@ def load_words(nc, words, dram_words, g, half):
     )
 
 
-def load_column_tile(nc, words, dram_words, n):
+def load_column_tile(nc, tiles, dram_words, n):
     int32_cols = slice(n * N_TILE // 2, (n + 1) * N_TILE // 2)
-    nc.sync.dma_start(
-        out=words[:].bitcast(I32),
-        in_=dram_words.bitcast(I32)[:, :, int32_cols].rearrange("g p c -> p g c"),
-    )
+    for i, words in enumerate(tiles):
+        groups = words.shape[1]
+        nc.sync.dma_start(
+            out=words[:].bitcast(I32),
+            in_=dram_words.bitcast(I32)[i * groups : (i + 1) * groups, :, int32_cols].rearrange(
+                "g p c -> p g c"
+            ),
+        )
 
 
-def copy_out(nc, b, out, in_):
-    if b == 0:
+def copy_out(nc, i, out, in_):
+    if i == 0:
         nc.vector.tensor_copy(out=out, in_=in_)
     else:
         nc.scalar.copy(out=out, in_=in_)
@@ -76,13 +80,12 @@ def copy_out(nc, b, out, in_):
 def mx_pass(nc, acc, codes, code_scales, words, planes, g, b, first):
     half, col = divmod(first, NL)
     width = acc.shape[-1]
-    tile, tile_first = words(first)
-    groups = tile.shape[1]
+    groups = codes.shape[1]
     nc.tensor.matmul_mx(
         out=acc,
         lhsT=codes[:, g, b, :].bitcast(FP8X4),
         lhsT_scale=code_scales[:, g, b, :],
-        rhs=tile[:, g, 2 * (first - tile_first) : 2 * (first - tile_first + width)].bitcast(FP4X4),
+        rhs=words(g, first, width).bitcast(FP4X4),
         rhs_scale=planes[half][:, g, col : col + width],
         start=(g == 0),
         stop=(g == groups - 1),
@@ -106,23 +109,26 @@ def tile_kktloss_pa_kernel(
         volt_scales = keep.tile([P, G1, B_TILES, P], U8, align_bytes=64)
         im_tile = keep.tile([P, G1, 2 * K2], U8, align_bytes=64)
 
-        def im_words(first):
-            return im_tile, 0
+        def im_words(g, first, width):
+            return im_tile[:, g, 2 * first : 2 * (first + width)]
 
         im_planes_0 = keep.tile([P, G1, NL], U8, align_bytes=64)
         im_planes_1 = keep.tile([P, G1, NL], U8, align_bytes=64)
         im_planes = [im_planes_0, im_planes_1]
         ybr_half = keep.tile([P, G2, 2 * NL], U8, align_bytes=64)
-        ybr_tile_3 = keep.tile([P, G2, 2 * N_TILE], U8, align_bytes=64)
+        ybr_tile_3a = keep.tile([P, G2 // 2, 2 * N_TILE], U8, align_bytes=64)
+        ybr_tile_3b = keep.tile([P, G2 // 2, 2 * N_TILE], U8, align_bytes=64)
         ybr_tile_4 = keep.tile([P, G2, 2 * N_TILE], U8, align_bytes=64)
         ybr_tile_5 = keep.tile([P, G2, 2 * N_TILE], U8, align_bytes=64)
-        ybr_tiles = {3: ybr_tile_3, 4: ybr_tile_4, 5: ybr_tile_5}
+        ybr_tiles = {3: [ybr_tile_3a, ybr_tile_3b], 4: [ybr_tile_4], 5: [ybr_tile_5]}
 
-        def ybr_words(first):
+        def ybr_words(g, first, width):
             n = first // N_TILE
-            if n in SECOND_HALF:
-                return ybr_tiles[n], N_TILE * n
-            return ybr_half, 0
+            if n not in SECOND_HALF:
+                return ybr_half[:, g, 2 * first : 2 * (first + width)]
+            groups = G2 // len(ybr_tiles[n])
+            col = first - N_TILE * n
+            return ybr_tiles[n][g // groups][:, g % groups, 2 * col : 2 * (col + width)]
 
         ybr_planes_0 = keep.tile([P, G2, NL], U8, align_bytes=64)
         ybr_planes_1 = keep.tile([P, G2, NL], U8, align_bytes=64)
@@ -211,26 +217,30 @@ def tile_kktloss_pa_kernel(
         def sort_d(n, b, acc):
             copy_out(nc, b, out=d_sorted[:, n, b], in_=acc[:].rearrange("r (p u e) -> r u p e", u=2, e=2))
 
-        def turn_and_quantise_d(n):
-            for b in range(B_TILES):
-                d_turned = turn_pool.tile([P, 2, P], F32, name="d_turned", tag="turn")
-                for u in range(2):
-                    nc.tensor.transpose(
-                        d_turned[:, u, :],
-                        d_sorted[:, n, b, u].rearrange("r p e -> r (p e)").bitcast(F32),
-                        ident_f32[:],
-                    )
+        def turn_and_quantise_d(tiles):
+            for i, n in enumerate(tiles):
+                d_turned = turn_pool.tile([P, B_TILES, 2, P], F32, name="d_turned", tag="turn")
+                for b in range(B_TILES):
+                    for u in range(2):
+                        nc.tensor.transpose(
+                            d_turned[:, b, u, :],
+                            d_sorted[:, n, b, u].rearrange("r p e -> r (p e)").bitcast(F32),
+                            ident_f32[:],
+                        )
                 copy_out(
                     nc,
-                    b,
-                    out=d_grouped[:, n, b].bitcast(F32),
-                    in_=d_turned[:].rearrange("p u r -> p r u"),
+                    i,
+                    out=d_grouped[:, n].bitcast(F32),
+                    in_=d_turned[:].rearrange("p b u r -> p b r u"),
                 )
-            nc.vector.quantize_mx(
-                out=d_codes[:, n].rearrange("p b r -> p (b r)").bitcast(FP8X4),
-                scales=d_scales[:, n].rearrange("p b r -> p (b r)"),
-                in_=d_grouped[:, n].rearrange("p b r t -> p (b r t)"),
-            )
+            for n in tiles:
+                nc.vector.quantize_mx(
+                    out=d_codes[:, n].rearrange("p b r -> p (b r)").bitcast(FP8X4),
+                    scales=d_scales[:, n].rearrange("p b r -> p (b r)"),
+                    in_=d_grouped[:, n].rearrange("p b r t -> p (b r t)"),
+                )
+
+        turns = {0: (0, 1), 2: (2,)}
 
         def open_banks(n_tiles):
             banks = {}
@@ -252,8 +262,8 @@ def tile_kktloss_pa_kernel(
             for n in SECOND_HALF[0:2]:
                 for b in range(B_TILES):
                     mx_pass(nc, acc[(n, b)][:], volt_codes, volt_scales, im_words, im_planes, g, b, N_TILE * n)
-            if g < HALF_TILES:
-                turn_and_quantise_d(g)
+            if g in turns:
+                turn_and_quantise_d([FIRST_HALF[i] for i in turns[g]])
         for n in SECOND_HALF[0:2]:
             for b in range(B_TILES):
                 sort_d(n, b, acc[(n, b)])
@@ -269,8 +279,8 @@ def tile_kktloss_pa_kernel(
             for n in FIRST_HALF:
                 for b in range(B_TILES):
                     mx_pass(nc, acc[(n, b)][:], d_codes, d_scales, ybr_words, ybr_planes, g, b, N_TILE * n)
-            if g < HALF_TILES:
-                turn_and_quantise_d(HALF_TILES + g)
+            if g in turns:
+                turn_and_quantise_d([SECOND_HALF[i] for i in turns[g]])
 
         for b in range(B_TILES):
             nc.scalar.activation(out=abs_mu[:, b, :], in_=mu_sb[:, b, :], func=ACT.Abs)
@@ -281,7 +291,7 @@ def tile_kktloss_pa_kernel(
                 scalar2=None,
                 op0=ALU.min,
                 op1=ALU.subtract,
-                accum_out=terms[:, b, TERMS - 1 : TERMS],
+                accum_out=terms[:, b, 0:1],
             )
 
         for n in FIRST_HALF:
@@ -290,8 +300,14 @@ def tile_kktloss_pa_kernel(
                 nc.scalar.activation(
                     out=excess[:, b, cols], in_=acc[(n, b)][:], func=ACT.Square, scale=SQRT_HALF
                 )
-                nc.vector.tensor_tensor(
-                    out=excess[:, b, cols], in0=excess[:, b, cols], in1=limit_sq[:, cols], op=ALU.subtract
+                nc.vector.scalar_tensor_tensor(
+                    out=excess[:, b, cols],
+                    in0=excess[:, b, cols],
+                    scalar=0.0,
+                    in1=limit_sq[:, cols],
+                    op0=ALU.add,
+                    op1=ALU.subtract,
+                    accum_out=terms[:, b, 1 + n : 2 + n],
                 )
 
         def add_absolute(weighted, width, b, term):
@@ -304,47 +320,50 @@ def tile_kktloss_pa_kernel(
                 accum_out=terms[:, b, term : term + 1],
             )
 
-        def pieces(n, b):
-            first = N_TILE * (n - HALF_TILES)
-            if (n, b) == (SECOND_HALF[-1], B_TILES - 1):
-                return [(first, N_TILE // 2, P), (first + N_TILE // 2, N_TILE // 2, P)]
-            return [(first, N_TILE, N_TILE)]
+        opened = {}
+        n = SECOND_HALF[0]
+        for b in range(B_TILES):
+            opened[(n, b)] = acc_pool.tile([P, N_TILE], F32, name="acc", tag="acc")
+            for g in range(G2 // 2):
+                mx_pass(nc, opened[(n, b)][:], d_codes, d_scales, ybr_words, ybr_planes, g, b, N_TILE * n)
 
-        next_term = [0] * B_TILES
+        def pieces(n, b):
+            if (n, b) == (SECOND_HALF[-1], B_TILES - 1):
+                return [slice(0, N_TILE // 2), slice(N_TILE // 2, N_TILE)]
+            return [slice(0, N_TILE)]
+
+        next_term = [1 + HALF_TILES] * B_TILES
         waiting = []
         for n in SECOND_HALF:
             for b in range(B_TILES):
-                for first, width, pass_width in pieces(n, b):
-                    cols = slice(first, first + width)
+                if (n, b) in opened:
+                    acc = opened[(n, b)]
+                    groups = range(G2 // 2, G2)
+                else:
                     acc = acc_pool.tile([P, N_TILE], F32, name="acc", tag="acc")
-                    for col in range(0, width, pass_width):
-                        for g in range(G2):
-                            mx_pass(
-                                nc,
-                                acc[:, col : col + pass_width],
-                                d_codes,
-                                d_scales,
-                                ybr_words,
-                                ybr_planes,
-                                g,
-                                b,
-                                NL + first + col,
-                            )
+                    groups = range(G2)
+                for g in groups:
+                    mx_pass(nc, acc[:], d_codes, d_scales, ybr_words, ybr_planes, g, b, N_TILE * n)
+                for piece in pieces(n, b):
+                    width = piece.stop - piece.start
+                    first = N_TILE * (n - HALF_TILES) + piece.start
+                    cols = slice(first, first + width)
                     term = next_term[b]
                     next_term[b] += 2
                     im_sq = work.tile([P, N_TILE], F32, name="im_sq")
                     nc.scalar.activation(
-                        out=im_sq[:, 0:width], in_=acc[:, 0:width], func=ACT.Square, scale=SQRT_HALF
+                        out=im_sq[:, 0:width],
+                        in_=acc[:, piece],
+                        func=ACT.Square,
+                        scale=SQRT_HALF,
+                        accum_out=terms[:, b, term : term + 1],
                     )
                     h_tile = work.tile([P, N_TILE], F32, name="h_tile")
-                    nc.vector.scalar_tensor_tensor(
+                    nc.vector.tensor_tensor(
                         out=h_tile[:, 0:width],
                         in0=im_sq[:, 0:width],
-                        scalar=0.0,
                         in1=excess[:, b, cols],
-                        op0=ALU.add,
-                        op1=ALU.add,
-                        accum_out=terms[:, b, term : term + 1],
+                        op=ALU.add,
                     )
                     weighted = work.tile([P, N_TILE], F32, name="weighted")
                     nc.vector.scalar_tensor_tensor(
@@ -358,8 +377,8 @@ def tile_kktloss_pa_kernel(
                     waiting.append((weighted, width, b, term + 1))
                     if len(waiting) > 2:
                         add_absolute(*waiting.pop(0))
-        for piece in waiting:
-            add_absolute(*piece)
+        for last in waiting:
+            add_absolute(*last)
 
         nc.vector.tensor_reduce(
             out=loss_cols[:, 0:B_TILES], in_=terms[:], axis=mybir.AxisListType.X, op=ALU.add

import math
from contextlib import ExitStack

import concourse.mybir as mybir
from concourse.masks import make_identity

F32 = mybir.dt.float32
BF16 = mybir.dt.bfloat16
I32 = mybir.dt.int32
U32 = mybir.dt.uint32
U8 = mybir.dt.uint8
FP8X4 = mybir.dt.float8_e4m3fn_x4
FP4X4 = mybir.dt.float4_e2m1fn_x4
ALU = mybir.AluOpType
ACT = mybir.ActivationFunctionType

P = 128
PACK = 4
K_GROUP = P * PACK
N_TILE = 512
B_TILES = 2
K1 = 2048
K2 = 3072
NL = 1536
G1 = K1 // K_GROUP
G2 = K2 // K_GROUP
HALF_TILES = NL // N_TILE
FIRST_HALF = range(0, HALF_TILES)
SECOND_HALF = range(HALF_TILES, 2 * HALF_TILES)

WARM_UP = 8
TURN = 32
TERMS = 12
SQRT_HALF = math.sqrt(0.5)

FLOPS = 2 * B_TILES * P * (K1 * K2 + K2 * 2 * NL)


def load_scale_planes(nc, planes, scales, half, groups_per_dma):
    groups = scales.shape[0]
    int32_cols = slice(half * NL // 4, (half + 1) * NL // 4)
    rows = scales.bitcast(I32).rearrange("g q n -> q g n")[:, :, int32_cols]
    for g0 in range(0, groups, groups_per_dma):
        for q in range(8):
            first = 32 * (q // 4) + q % 4
            nc.sync.dma_start(
                out=planes[first:P:64, g0 : g0 + groups_per_dma, :].bitcast(I32),
                in_=rows[q:16:8, g0 : g0 + groups_per_dma, :],
            )


def load_words(nc, words, dram_words, g, half):
    int32_cols = slice(half * NL // 2, (half + 1) * NL // 2)
    byte_cols = slice(half * NL * 2, (half + 1) * NL * 2)
    nc.sync.dma_start(
        out=words[:, g, byte_cols].bitcast(I32),
        in_=dram_words.bitcast(I32)[g, :, int32_cols],
    )


def load_column_tile(nc, tiles, dram_words, n):
    int32_cols = slice(n * N_TILE // 2, (n + 1) * N_TILE // 2)
    for i, words in enumerate(tiles):
        groups = words.shape[1]
        nc.sync.dma_start(
            out=words[:].bitcast(I32),
            in_=dram_words.bitcast(I32)[i * groups : (i + 1) * groups, :, int32_cols].rearrange(
                "g p c -> p g c"
            ),
        )


def copy_out(nc, i, out, in_):
    if i == 0:
        nc.vector.tensor_copy(out=out, in_=in_)
    else:
        nc.scalar.copy(out=out, in_=in_)


def mx_pass(nc, acc, codes, code_scales, words, planes, g, b, first):
    half, col = divmod(first, NL)
    width = acc.shape[-1]
    groups = codes.shape[1]
    nc.tensor.matmul_mx(
        out=acc,
        lhsT=codes[:, g, b, :].bitcast(FP8X4),
        lhsT_scale=code_scales[:, g, b, :],
        rhs=words(g, first, width).bitcast(FP4X4),
        rhs_scale=planes[half][:, g, col : col + width],
        start=(g == 0),
        stop=(g == groups - 1),
    )


def tile_kktloss_pa_kernel(
    tc, Volt, IM_words, IM_scales, Ybr_words, Ybr_scales, L_limit, n_o_mu_i_u, out
):
    nc = tc.nc
    with ExitStack() as ctx:
        keep = ctx.enter_context(tc.tile_pool(name="keep", bufs=1))
        work = ctx.enter_context(tc.tile_pool(name="work", bufs=3))
        acc_pool = ctx.enter_context(tc.psum_pool(name="acc", bufs=6))
        turn_pool = ctx.enter_context(tc.psum_pool(name="turn", bufs=2))
        ctx.enter_context(tc.manual_schedule())

        volt_sb = keep.tile([P, B_TILES, K1], BF16)
        volt_grouped = keep.tile([P, G1, B_TILES, P, PACK], BF16, align_bytes=64)
        volt_codes = keep.tile([P, G1, B_TILES, P], U32, align_bytes=64)
        volt_scales = keep.tile([P, G1, B_TILES, P], U8, align_bytes=64)
        im_tile = keep.tile([P, G1, 2 * K2], U8, align_bytes=64)

        def im_words(g, first, width):
            return im_tile[:, g, 2 * first : 2 * (first + width)]

        im_planes_0 = keep.tile([P, G1, NL], U8, align_bytes=64)
        im_planes_1 = keep.tile([P, G1, NL], U8, align_bytes=64)
        im_planes = [im_planes_0, im_planes_1]
        ybr_half = keep.tile([P, G2, 2 * NL], U8, align_bytes=64)
        ybr_tile_3a = keep.tile([P, G2 // 2, 2 * N_TILE], U8, align_bytes=64)
        ybr_tile_3b = keep.tile([P, G2 // 2, 2 * N_TILE], U8, align_bytes=64)
        ybr_tile_4 = keep.tile([P, G2, 2 * N_TILE], U8, align_bytes=64)
        ybr_tile_5 = keep.tile([P, G2, 2 * N_TILE], U8, align_bytes=64)
        ybr_tiles = {3: [ybr_tile_3a, ybr_tile_3b], 4: [ybr_tile_4], 5: [ybr_tile_5]}

        def ybr_words(g, first, width):
            n = first // N_TILE
            if n not in SECOND_HALF:
                return ybr_half[:, g, 2 * first : 2 * (first + width)]
            groups = G2 // len(ybr_tiles[n])
            col = first - N_TILE * n
            return ybr_tiles[n][g // groups][:, g % groups, 2 * col : 2 * (col + width)]

        ybr_planes_0 = keep.tile([P, G2, NL], U8, align_bytes=64)
        ybr_planes_1 = keep.tile([P, G2, NL], U8, align_bytes=64)
        ybr_planes = [ybr_planes_0, ybr_planes_1]
        d_sorted = keep.tile([P, G2, B_TILES, 2, P, 2], BF16)
        d_grouped = keep.tile([P, G2, B_TILES, P, PACK], BF16, align_bytes=64)
        d_codes = keep.tile([P, G2, B_TILES, P], U32, align_bytes=64)
        d_scales = keep.tile([P, G2, B_TILES, P], U8, align_bytes=64)
        limit_rows = keep.tile([P, NL], BF16)
        limit_sq = keep.tile([P, NL], F32)
        mu_sb = keep.tile([P, B_TILES, NL], BF16)
        abs_mu = keep.tile([P, B_TILES, NL], BF16)
        min_mu = keep.tile([P, NL], F32)
        excess = keep.tile([P, B_TILES, NL], F32)
        ones = keep.tile([P, N_TILE], BF16)
        ident_f32 = keep.tile([P, P], F32)
        terms = keep.tile([P, B_TILES, TERMS], F32)
        loss_cols = keep.tile([P, TURN], F32, align_bytes=64)
        loss_rows = keep.tile([P, TURN], F32, align_bytes=64)

        nc.vector.memset(ones[:], 1.0)
        for planes in im_planes:
            nc.vector.memset(planes[:].rearrange("p g n -> p (g n)").bitcast(I32), 0)
        nc.gpsimd.memset(limit_rows[:].bitcast(I32), 0)
        make_identity(nc, ident_f32[:])
        nc.gpsimd.memset(loss_cols[:], 0.0)
        nc.gpsimd.memset(terms[:], 0.0)

        nc.sync.dma_start(out=volt_sb[:], in_=Volt.rearrange("(b p) k -> p b k", p=P))
        nc.sync.dma_start(out=limit_rows[0:1, :], in_=L_limit.rearrange("(o l) -> o l", o=1))
        for half in range(2):
            load_scale_planes(nc, im_planes[half], IM_scales, half, groups_per_dma=G1)
            for g in range(G1):
                load_words(nc, im_tile, IM_words, g, half)

        for i in range(WARM_UP):
            warm = turn_pool.tile([P, N_TILE], F32, name="warm", tag="turn")
            nc.tensor.matmul(out=warm[:], lhsT=ones[:, 0:P], rhs=ones[:], start=True, stop=True)

        def spread_limit(n):
            cols = slice(N_TILE * n, N_TILE * (n + 1))
            spread = turn_pool.tile([P, N_TILE], F32, name="spread", tag="turn")
            nc.tensor.matmul(out=spread[:], lhsT=ones[:, 0:P], rhs=limit_rows[:, cols], start=True, stop=True)
            nc.scalar.activation(out=limit_sq[:, cols], in_=spread[:], func=ACT.Square, scale=SQRT_HALF)

        volt_as_words = volt_sb[:].bitcast(F32)

        def quantise_volt(g):
            nc.vector.quantize_mx(
                out=volt_codes[:, g].rearrange("p b r -> p (b r)").bitcast(FP8X4),
                scales=volt_scales[:, g].rearrange("p b r -> p (b r)"),
                in_=volt_grouped[:, g].rearrange("p b r t -> p (b r t)"),
            )

        for g in range(G1):
            for b in range(B_TILES):
                volt_turned = acc_pool.tile([P, 2, P], F32, name="volt_turned", tag="acc")
                for u in range(2):
                    nc.tensor.transpose(
                        volt_turned[:, u, :],
                        volt_as_words[:, b, 256 * g + u : 256 * (g + 1) : 2],
                        ident_f32[:],
                    )
                copy_out(
                    nc,
                    b,
                    out=volt_grouped[:, g, b].bitcast(F32),
                    in_=volt_turned[:].rearrange("p u r -> p r u"),
                )
            if g > 0:
                quantise_volt(g - 1)
            if g in FIRST_HALF:
                spread_limit(g)
        quantise_volt(G1 - 1)
        for planes in ybr_planes:
            nc.vector.memset(planes[:].rearrange("p g n -> p (g n)").bitcast(I32), 0)

        load_scale_planes(nc, ybr_planes[0], Ybr_scales, 0, groups_per_dma=G2)
        for g in range(G2):
            load_words(nc, ybr_half, Ybr_words, g, 0)
        nc.sync.dma_start(out=mu_sb[:], in_=n_o_mu_i_u.rearrange("(b p) l -> p b l", p=P))
        load_scale_planes(nc, ybr_planes[1], Ybr_scales, 1, groups_per_dma=G2)
        for n in SECOND_HALF:
            load_column_tile(nc, ybr_tiles[n], Ybr_words, n)

        def sort_d(n, b, acc):
            copy_out(nc, b, out=d_sorted[:, n, b], in_=acc[:].rearrange("r (p u e) -> r u p e", u=2, e=2))

        def turn_and_quantise_d(tiles):
            for i, n in enumerate(tiles):
                d_turned = turn_pool.tile([P, B_TILES, 2, P], F32, name="d_turned", tag="turn")
                for b in range(B_TILES):
                    for u in range(2):
                        nc.tensor.transpose(
                            d_turned[:, b, u, :],
                            d_sorted[:, n, b, u].rearrange("r p e -> r (p e)").bitcast(F32),
                            ident_f32[:],
                        )
                copy_out(
                    nc,
                    i,
                    out=d_grouped[:, n].bitcast(F32),
                    in_=d_turned[:].rearrange("p b u r -> p b r u"),
                )
            for n in tiles:
                nc.vector.quantize_mx(
                    out=d_codes[:, n].rearrange("p b r -> p (b r)").bitcast(FP8X4),
                    scales=d_scales[:, n].rearrange("p b r -> p (b r)"),
                    in_=d_grouped[:, n].rearrange("p b r t -> p (b r t)"),
                )

        turns = {0: (0, 1), 2: (2,)}

        def open_banks(n_tiles):
            banks = {}
            for n in n_tiles:
                for b in range(B_TILES):
                    banks[(n, b)] = acc_pool.tile([P, N_TILE], F32, name="acc", tag="acc")
            return banks

        acc = open_banks(FIRST_HALF)
        for g in range(G1):
            for n in FIRST_HALF:
                for b in range(B_TILES):
                    mx_pass(nc, acc[(n, b)][:], volt_codes, volt_scales, im_words, im_planes, g, b, N_TILE * n)
        for n in FIRST_HALF:
            for b in range(B_TILES):
                sort_d(n, b, acc[(n, b)])
        acc = open_banks(SECOND_HALF[0:2])
        for g in range(G1):
            for n in SECOND_HALF[0:2]:
                for b in range(B_TILES):
                    mx_pass(nc, acc[(n, b)][:], volt_codes, volt_scales, im_words, im_planes, g, b, N_TILE * n)
            if g in turns:
                turn_and_quantise_d([FIRST_HALF[i] for i in turns[g]])
        for n in SECOND_HALF[0:2]:
            for b in range(B_TILES):
                sort_d(n, b, acc[(n, b)])
        n = SECOND_HALF[2]
        acc = open_banks([n])
        for b in range(B_TILES):
            for g in range(G1):
                mx_pass(nc, acc[(n, b)][:], volt_codes, volt_scales, im_words, im_planes, g, b, N_TILE * n)
            sort_d(n, b, acc[(n, b)])

        acc = open_banks(FIRST_HALF)
        for g in range(G2):
            for n in FIRST_HALF:
                for b in range(B_TILES):
                    mx_pass(nc, acc[(n, b)][:], d_codes, d_scales, ybr_words, ybr_planes, g, b, N_TILE * n)
            if g in turns:
                turn_and_quantise_d([SECOND_HALF[i] for i in turns[g]])

        for b in range(B_TILES):
            nc.scalar.activation(out=abs_mu[:, b, :], in_=mu_sb[:, b, :], func=ACT.Abs)
            nc.vector.tensor_scalar(
                out=min_mu[:],
                in0=mu_sb[:, b, :],
                scalar1=0.0,
                scalar2=None,
                op0=ALU.min,
                op1=ALU.subtract,
                accum_out=terms[:, b, 0:1],
            )

        for n in FIRST_HALF:
            cols = slice(N_TILE * n, N_TILE * (n + 1))
            for b in range(B_TILES):
                nc.scalar.activation(
                    out=excess[:, b, cols], in_=acc[(n, b)][:], func=ACT.Square, scale=SQRT_HALF
                )
                nc.vector.scalar_tensor_tensor(
                    out=excess[:, b, cols],
                    in0=excess[:, b, cols],
                    scalar=0.0,
                    in1=limit_sq[:, cols],
                    op0=ALU.add,
                    op1=ALU.subtract,
                    accum_out=terms[:, b, 1 + n : 2 + n],
                )

        def add_absolute(weighted, width, b, term):
            absolute = work.tile([P, N_TILE], F32, name="absolute")
            nc.scalar.activation(
                out=absolute[:, 0:width],
                in_=weighted[:, 0:width],
                func=ACT.Abs,
                scale=2.0,
                accum_out=terms[:, b, term : term + 1],
            )

        opened = {}
        n = SECOND_HALF[0]
        for b in range(B_TILES):
            opened[(n, b)] = acc_pool.tile([P, N_TILE], F32, name="acc", tag="acc")
            for g in range(G2 // 2):
                mx_pass(nc, opened[(n, b)][:], d_codes, d_scales, ybr_words, ybr_planes, g, b, N_TILE * n)

        def pieces(n, b):
            if (n, b) == (SECOND_HALF[-1], B_TILES - 1):
                return [slice(0, N_TILE // 2), slice(N_TILE // 2, N_TILE)]
            return [slice(0, N_TILE)]

        next_term = [1 + HALF_TILES] * B_TILES
        waiting = []
        for n in SECOND_HALF:
            for b in range(B_TILES):
                if (n, b) in opened:
                    acc = opened[(n, b)]
                    groups = range(G2 // 2, G2)
                else:
                    acc = acc_pool.tile([P, N_TILE], F32, name="acc", tag="acc")
                    groups = range(G2)
                for g in groups:
                    mx_pass(nc, acc[:], d_codes, d_scales, ybr_words, ybr_planes, g, b, N_TILE * n)
                for piece in pieces(n, b):
                    width = piece.stop - piece.start
                    first = N_TILE * (n - HALF_TILES) + piece.start
                    cols = slice(first, first + width)
                    term = next_term[b]
                    next_term[b] += 2
                    im_sq = work.tile([P, N_TILE], F32, name="im_sq")
                    nc.scalar.activation(
                        out=im_sq[:, 0:width],
                        in_=acc[:, piece],
                        func=ACT.Square,
                        scale=SQRT_HALF,
                        accum_out=terms[:, b, term : term + 1],
                    )
                    h_tile = work.tile([P, N_TILE], F32, name="h_tile")
                    nc.vector.tensor_tensor(
                        out=h_tile[:, 0:width],
                        in0=im_sq[:, 0:width],
                        in1=excess[:, b, cols],
                        op=ALU.add,
                    )
                    weighted = work.tile([P, N_TILE], F32, name="weighted")
                    nc.vector.scalar_tensor_tensor(
                        out=weighted[:, 0:width],
                        in0=abs_mu[:, b, cols],
                        scalar=0.5,
                        in1=h_tile[:, 0:width],
                        op0=ALU.add,
                        op1=ALU.mult,
                    )
                    waiting.append((weighted, width, b, term + 1))
                    if len(waiting) > 2:
                        add_absolute(*waiting.pop(0))
        for last in waiting:
            add_absolute(*last)

        nc.vector.tensor_reduce(
            out=loss_cols[:, 0:B_TILES], in_=terms[:], axis=mybir.AxisListType.X, op=ALU.add
        )
        nc.vector.transpose(out=loss_rows[:], in_=loss_cols[:])
        out_runs = out.rearrange("(b q r) -> b q r", b=B_TILES, r=TURN)
        for b in range(B_TILES):
            nc.sync.dma_start(out=out_runs[b], in_=loss_rows[b:P:TURN, :])
